import numpy as np
import ml_dtypes


def mxq(x, axis, fmt="e4m3"):
    dtype, down = {"e4m3": (ml_dtypes.float8_e4m3fn, 7), "e5m2": (ml_dtypes.float8_e5m2, 14)}[fmt]
    v = np.moveaxis(np.asarray(x, np.float32).astype(ml_dtypes.bfloat16).astype(np.float64), axis, -1)
    blocks = v.reshape(v.shape[:-1] + (-1, 32))
    amax = np.abs(blocks).max(-1, keepdims=True)
    byte = np.maximum(np.where(amax > 0, np.frexp(amax)[1] - 1 + 127, 0) - down, 1)
    scale = np.exp2(byte - 127.0)
    codes = (blocks / scale).astype(np.float32).astype(dtype).astype(np.float64)
    return np.moveaxis((codes * scale).reshape(v.shape), -1, axis)


WIDE = False


def mx_kscale(k):
    if not WIDE:
        return np.ones(k)
    levels = np.array([10, -10, 5, -5, 0])
    if k % 512:
        return np.exp2(np.random.permutation(np.resize(levels, k // 32))).repeat(32)
    a = np.empty((k // 512, 16))
    for p in range(k // 512):
        a[p, :8] = np.random.permutation(np.resize(levels, 8))
        for g in range(8):
            far = levels[np.abs(levels - a[p, g]) >= 10]
            a[p, g + 8] = far[np.random.randint(len(far))]
    return np.exp2(a.ravel()).repeat(32)


BF16 = ml_dtypes.bfloat16


def bf(x):
    return np.asarray(x, np.float32).astype(BF16)


def f64(x):
    return np.asarray(x).astype(np.float64)


B, IN, HID, OUT, LAYERS, NG = 1024, 512, 1024, 512, 2, 4
GW = NG * HID


def sigmoid(v):
    return 1.0 / (1.0 + np.exp(-v))


def setup_inputs():
    s = mx_kscale(IN)
    return {
        "regime_vector": bf(np.random.standard_normal((B, IN)) * s),
        "W_ih0": bf(np.random.standard_normal((GW, IN)) / np.sqrt(IN) / s),
        "hh_gates": bf(np.random.standard_normal(GW) * 0.5),
        "b_ih0": bf(np.random.standard_normal(GW) * 0.3),
        "b_hh0": bf(np.random.standard_normal(GW) * 0.3),
        "c_init": bf(np.random.standard_normal(HID)),
    }


def core(regime_vector, W_ih0, hh_gates, b_ih0, b_hh0, c_init):
    gates = (mxq(f64(regime_vector), 1, "e4m3") @ mxq(f64(W_ih0).T, 0, "e4m3")) + f64(hh_gates) + (f64(b_ih0) + f64(b_hh0))
    i, f, g, o = np.split(gates, NG, axis=-1)
    i, f, o = sigmoid(i), sigmoid(f), sigmoid(o)
    g = np.tanh(g)
    c_new = f * f64(c_init) + i * g
    return o * np.tanh(c_new)


def e4m3fn_bytes(y):
    return np.clip(np.asarray(y, np.float64), -448.0, 448.0).astype(np.float32).astype(ml_dtypes.float8_e4m3fn).view(np.uint8)


def reference(regime_vector, W_ih0, hh_gates, b_ih0, b_hh0, c_init):
    out = core(regime_vector, W_ih0, hh_gates, b_ih0, b_hh0, c_init)
    s = np.max(np.abs(out), axis=-1, keepdims=True) / 448.0
    return out, e4m3fn_bytes(out / s)

@@ -1,0 +1,328 @@
+from contextlib import ExitStack
+
+import concourse.mybir as mybir
+from concourse.masks import make_identity
+
+F32 = mybir.dt.float32
+BF16 = mybir.dt.bfloat16
+U32 = mybir.dt.uint32
+U8 = mybir.dt.uint8
+FP8 = mybir.dt.float8_e4m3fn
+FP8X4 = mybir.dt.float8_e4m3fn_x4
+ACT = mybir.ActivationFunctionType
+ALU = mybir.AluOpType
+AX = mybir.AxisListType
+
+B, IN, HID = 1024, 512, 1024
+FLOPS = 2 * B * 4 * HID * IN
+
+P = 128
+NB = 2
+NH = 8
+NJ = 4
+CH = 512
+GATE_OF_POS = (0, 2, 1, 3)
+
+STEPS = [(0, 0), (1, 0), (0, 1), (1, 1), (0, 2), (1, 2), (0, 3), (0, 4), (1, 3), (0, 5), (0, 6), (1, 4), (0, 7), (1, 5), (1, 6), (1, 7)]
+BOUNDS = (0, 4, 7, 8)
+RD_BOUNDS = (0, 4, 6, 7, 8)
+N_FINE = 3
+N_HEAD = 3
+PC_ON_SCALAR = (0, 1, 2, 3, 4, 5, 6)
+CAST_ON_SCALAR = ((0, 2, 0), (0, 2, 1), (0, 2, 2), (0, 3, 0), (0, 3, 1), (0, 3, 2), (1, 0, 1), (1, 1, 1), (1, 2, 1), (1, 3, 1))
+RD_POPS = 1024
+CAST_POPS = 3
+CAST_STOP = 1
+N_WARM_END = 2
+LEAD = 4
+SMALL_DMA_AFTER = 2
+SMALL_AFTER = 4
+WARM_UNTIL = 6
+N_WARM = 6
+WARM_EVERY = 2
+
+
+def tile_rdecommunicationlstm_pa_kernel(tc, regime_vector, W_ih0, hh_gates, b_ih0, b_hh0, c_init, out_0, out_1):
+    nc = tc.nc
+    n = len(STEPS)
+    with ExitStack() as ctx:
+        const = ctx.enter_context(tc.tile_pool(name="const", bufs=1))
+        keep = ctx.enter_context(tc.tile_pool(name="keep", bufs=1))
+        work = ctx.enter_context(tc.tile_pool(name="work", bufs=3))
+        gates = ctx.enter_context(tc.psum_pool(name="gates", bufs=1))
+        turn = ctx.enter_context(tc.psum_pool(name="turn", bufs=4))
+        ctx.enter_context(tc.manual_schedule())
+
+        units, first_use = [], {}
+        for s in range(n):
+            for u in (("x", STEPS[s][0]), ("w", STEPS[s][1])):
+                if u not in units:
+                    units.append(u)
+                    first_use[u] = s
+        pieces = []
+        for i in range(len(units)):
+            nt = 1 if i < N_FINE else 2
+            pieces.extend([(units[i], t0, nt) for t0 in range(0, 4, nt)])
+        n_head = 4 * N_FINE + 2 * (N_HEAD - N_FINE)
+
+        xv = regime_vector.rearrange("(b f t p) k -> b f p t k", b=NB, f=2, t=2, p=P)
+        wv = W_ih0.rearrange("(t f h p) k -> h f p t k", t=2, f=2, h=NH, p=P)
+        vrows = const.tile([P, P], BF16, name="vrows")
+        nc.vector.memset(vrows[96:128, :], 0.0)
+        raw = {}
+        for pc in pieces:
+            if pieces.index(pc) == SMALL_DMA_AFTER:
+                nc.sync.dma_start(out=vrows[0:32, :], in_=hh_gates.rearrange("(c p) -> c p", p=P))
+                nc.sync.dma_start(out=vrows[32:64, :], in_=b_ih0.rearrange("(c p) -> c p", p=P))
+                nc.sync.dma_start(out=vrows[64:96, :], in_=b_hh0.rearrange("(c p) -> c p", p=P))
+                nc.sync.dma_start(out=vrows[96:104, :], in_=c_init.rearrange("(c p) -> c p", p=P))
+            u, t0, nt = pc
+            r = keep.tile([P, nt, IN], BF16, name="raw_%s%d_%d" % (u[0], u[1], t0))
+            view = xv if u[0] == "x" else wv
+            nc.sync.dma_start(out=r[:], in_=view[u[1], t0 // 2, :, t0 % 2 : t0 % 2 + nt, :])
+            raw[pc] = r
+
+        wz = const.tile([P, CH], BF16, name="wz")
+        nc.vector.memset(wz[:], 0.0)
+        wbank = gates.tile([P, CH], F32, name="wbank", tag="gate3")
+
+        def warm_pass():
+            nc.tensor.matmul(out=wbank[:], lhsT=wz[:, 0:P], rhs=wz[:], start=True, stop=True)
+
+        for i in range(N_WARM):
+            warm_pass()
+        zero = const.tile([P, 1], F32, name="zero")
+        nc.vector.memset(zero[:], 0.0)
+        warm = const.tile([P, 1], F32, name="warm")
+        nc.scalar.activation(out=warm[:], in_=zero[:], func=ACT.Sigmoid)
+        ident = const.tile([P, P], F32, name="ident")
+        make_identity(nc, ident[:])
+        ident_bf = const.tile([P, P], BF16, name="ident_bf")
+        make_identity(nc, ident_bf[:])
+        vcols = const.tile([P, P], F32, name="vcols")
+        bsum = const.tile([P, 32], F32, name="bsum")
+        bias = const.tile([P, 32], F32, name="bias")
+
+        def small_vectors():
+            bank = turn.tile([P, P], BF16, name="vbank", tag="turn")
+            nc.tensor.transpose(out=bank[:], in_=vrows[:], identity=ident_bf[:])
+            nc.vector.tensor_copy(out=vcols[:], in_=bank[:])
+            nc.vector.tensor_tensor(out=bsum[:], in0=vcols[:, 32:64], in1=vcols[:, 64:96], op=ALU.add)
+            nc.vector.tensor_tensor(out=bias[:], in0=bsum[:], in1=vcols[:, 0:32], op=ALU.add)
+
+        grouped, codes, scales, banks = {}, {}, {}, {}
+        for u in units:
+            codes[u] = keep.tile([P, CH], U32, name="codes_%s%d" % u, align_bytes=64)
+            scales[u] = keep.tile([P, CH], U8, name="scales_%s%d" % u, align_bytes=64)
+
+        def prep_turn(pc):
+            nt = pc[2]
+            bank = turn.tile([P, 2, nt, P], F32, name="pbank", tag="turn")
+            words = raw[pc][:].rearrange("p t k -> p (t k)").bitcast(F32)
+            for t in range(nt):
+                for w in range(2):
+                    nc.tensor.transpose(out=bank[:, w, t, :], in_=words[:, 256 * t + w : 256 * (t + 1) : 2], identity=ident[:])
+            banks[pc] = bank
+
+        def prep_copy(pc):
+            g = work.tile([P, pc[2] * CH], BF16, name="grouped", tag="grouped", bufs=4, align_bytes=64)
+            dst = g[:].bitcast(F32).rearrange("p (n w) -> p n w", w=2)
+            src = banks[pc][:].rearrange("p w t r -> p (t r) w")
+            if pieces.index(pc) in PC_ON_SCALAR:
+                nc.scalar.copy(out=dst, in_=src)
+            else:
+                nc.vector.tensor_copy(out=dst, in_=src)
+            grouped[pc] = g
+
+        def prep_quant(pc):
+            u, t0, nt = pc
+            cols = slice(P * t0, P * (t0 + nt))
+            nc.vector.quantize_mx(out=codes[u][:, cols].bitcast(FP8X4), scales=scales[u][:, cols], in_=grouped[pc][:])
+
+        nk = len(BOUNDS) - 1
+        nr = len(RD_BOUNDS) - 1
+        big = [[keep.tile([P, NJ, P * (BOUNDS[k + 1] - BOUNDS[k])], F32, name="big%d_%d" % (b, k)) for k in range(nk)] for b in range(NB)]
+        o8 = [[keep.tile([P, HID], FP8, name="o8_%d_%d" % (b, j)) for j in range(NJ)] for b in range(NB)]
+        stats = [keep.tile([P, nr, NJ], F32, name="stats%d" % b) for b in range(NB)]
+        rscale = [keep.tile([P, NJ], F32, name="rscale%d" % b) for b in range(NB)]
+        amax = [keep.tile([P, NJ], F32, name="amax%d" % b) for b in range(NB)]
+        qscale = [keep.tile([P, NJ], F32, name="qscale%d" % b) for b in range(NB)]
+        early = [keep.tile([P, NJ], F32, name="early%d" % b) for b in range(NB)]
+        o0v = out_0.rearrange("(b j p) c -> b p j c", b=NB, j=NJ, p=P)
+        o1v = out_1.rearrange("(b j p) c -> b j p c", b=NB, j=NJ, p=P)
+        pg, av, cv, tv = {}, {}, {}, {}
+
+        def mm(s, pos):
+            b, h = STEPS[s]
+            g = gates.tile([P, CH], F32, name="gate", tag="gate%d" % pos)
+            cols = slice(P * pos, P * (pos + 1))
+            nc.tensor.matmul_mx(out=g[:], lhsT=codes[("w", h)][:, cols].bitcast(FP8X4), lhsT_scale=scales[("w", h)][:, cols],
+                                rhs=codes[("x", b)][:].bitcast(FP8X4), rhs_scale=scales[("x", b)][:], start=True, stop=True)
+            pg[(s, pos)] = g
+
+        def act(s, pos):
+            b, h = STEPS[s]
+            a = work.tile([P, CH], F32, name="act", tag="act%d" % pos)
+            col = GATE_OF_POS[pos] * NH + h
+            nc.scalar.activation(out=a[:], in_=pg[(s, pos)][:], func=(ACT.Tanh if pos == 1 else ACT.Sigmoid), bias=bias[:, col : col + 1], scale=1.0)
+            av[(s, pos)] = a
+
+        def cell_ig(s):
+            ig = work.tile([P, CH], F32, name="ig", tag="ig")
+            nc.gpsimd.tensor_tensor(out=ig[:], in0=av[(s, 0)][:], in1=av[(s, 1)][:], op=ALU.mult)
+            cv[(s, "ig")] = ig
+
+        def cell_c(s):
+            b, h = STEPS[s]
+            c = work.tile([P, CH], F32, name="c", tag="c")
+            nc.vector.scalar_tensor_tensor(out=c[:], in0=av[(s, 2)][:], scalar=vcols[:, 96 + h : 97 + h], in1=cv[(s, "ig")][:], op0=ALU.mult, op1=ALU.add)
+            cv[(s, "c")] = c
+
+        def tail_turn(s):
+            for key, src in (("cT", cv[(s, "c")]), ("oT", av[(s, 3)])):
+                bank = turn.tile([P, NJ, P], F32, name="tbank", tag="turn")
+                for j in range(NJ):
+                    nc.tensor.transpose(out=bank[:, j, :], in_=src[:, P * j : P * (j + 1)], identity=ident[:])
+                tv[(s, key)] = bank
+
+        def tail_tanh(s):
+            th = work.tile([P, CH], F32, name="th", tag="th")
+            nc.scalar.activation(out=th[:], in_=tv[(s, "cT")][:].rearrange("p j c -> p (j c)"), func=ACT.Tanh)
+            tv[(s, "th")] = th
+
+        rdq, cq, sq = [], [], []
+        cur = {"rd": 0, "cast": 0, "scast": 0}
+        cast_count = {}
+
+        def tail_prod(s):
+            b, h = STEPS[s]
+            k = max([i for i in range(nk) if BOUNDS[i] <= h])
+            at = P * (h - BOUNDS[k])
+            nc.vector.tensor_tensor(out=big[b][k][:, :, at : at + P], in0=tv[(s, "oT")][:], in1=tv[(s, "th")][:].rearrange("p (j c) -> p j c", j=NJ), op=ALU.mult)
+            if h + 1 in RD_BOUNDS:
+                m = RD_BOUNDS.index(h + 1) - 1
+                if RD_BOUNDS[m] == BOUNDS[k] and h + 1 == BOUNDS[k + 1] and h + 1 - BOUNDS[k] == 1:
+                    rdq.append((b, NJ, m, k))
+                else:
+                    rdq.extend([(b, j, m, k) for j in range(NJ)])
+            if h + 1 in BOUNDS:
+                nc.sync.dma_start(out=o0v[b, :, :, P * BOUNDS[k] : P * BOUNDS[k + 1]], in_=big[b][k][:])
+
+        def do_rd(budget):
+            spent = 0
+            for i in range(len(rdq)):
+                if cur["rd"] >= len(rdq):
+                    return
+                b, j, m, k = rdq[cur["rd"]]
+                lo, hi = P * (RD_BOUNDS[m] - BOUNDS[k]), P * (RD_BOUNDS[m + 1] - BOUNDS[k])
+                spent += (hi - lo) * (NJ if j == NJ else 1)
+                if spent > budget:
+                    return
+                cur["rd"] += 1
+                if j == NJ:
+                    nc.vector.tensor_reduce(out=stats[b][:, m, :], in_=big[b][k][:], axis=AX.X, op=ALU.max, apply_absolute_value=True)
+                else:
+                    nc.vector.tensor_reduce(out=stats[b][:, m, j : j + 1], in_=big[b][k][:, j, lo:hi], axis=AX.X, op=ALU.max, apply_absolute_value=True)
+                if m == nr - 2 and j >= NJ - 1:
+                    nc.vector.tensor_reduce(out=amax[b][:], in_=stats[b][:, 0 : nr - 1, :].rearrange("p m j -> p j m"), axis=AX.X, op=ALU.max)
+                    nc.vector.tensor_scalar(out=early[b][:], in0=amax[b][:], scalar1=1.0 / 448.0, scalar2=None, op0=ALU.mult)
+                if m == nr - 1 and j >= NJ - 1:
+                    nc.vector.scalar_tensor_tensor(out=qscale[b][:], in0=stats[b][:, nr - 1, :], scalar=1.0 / 448.0, in1=early[b][:], op0=ALU.mult, op1=ALU.max)
+                    nc.vector.reciprocal(out=rscale[b][:], in_=qscale[b][:])
+                    for jj in range(NJ):
+                        for kk in range(nk):
+                            (sq if (b, jj, kk) in CAST_ON_SCALAR else cq).append((b, jj, kk))
+
+        def do_cast(count, queue, key):
+            for i in range(count):
+                if cur[key] >= len(queue):
+                    return
+                b, j, k = queue[cur[key]]
+                cur[key] += 1
+                dst = o8[b][j][:, P * BOUNDS[k] : P * BOUNDS[k + 1]]
+                if key == "scast":
+                    nc.scalar.activation(out=dst, in_=big[b][k][:, j, :], func=ACT.Identity, scale=rscale[b][:, j : j + 1], bias=zero[:, 0:1], saturate=False)
+                else:
+                    nc.vector.tensor_scalar(out=dst, in0=big[b][k][:, j, :], scalar1=rscale[b][:, j : j + 1], scalar2=None, op0=ALU.mult, saturate=False)
+                cast_count[(b, j)] = cast_count.get((b, j), 0) + 1
+                if cast_count[(b, j)] == nk:
+                    nc.sync.dma_start(out=o1v[b, j, :, :], in_=o8[b][j][:].bitcast(U8))
+
+        head = pieces[:n_head]
+        for i in range(n_head + 2):
+            if i < n_head:
+                prep_turn(head[i])
+                if i < WARM_UNTIL and i % WARM_EVERY == WARM_EVERY - 1:
+                    warm_pass()
+            if 1 <= i <= n_head:
+                prep_copy(head[i - 1])
+            if i >= 2:
+                prep_quant(head[i - 2])
+            if i == SMALL_AFTER:
+                small_vectors()
+            if i == 7:
+                mm(0, 0)
+                mm(0, 1)
+            if i == 11:
+                mm(0, 2)
+                mm(0, 3)
+
+        plan = {}
+        for pc in pieces[n_head:]:
+            plan.setdefault(first_use[pc[0]] - LEAD + pc[1] // 2, []).append(pc)
+        first_round = min([0] + [r for r in plan])
+
+        for r in range(first_round, n):
+            live = r >= 0
+            last = r == n - 1
+            if live:
+                act(r, 0)
+                act(r, 1)
+            if live and not last:
+                mm(r + 1, 0)
+                mm(r + 1, 1)
+            if live:
+                cell_ig(r)
+            if last:
+                tail_turn(r - 1)
+            if r > 1:
+                tail_tanh(r - 2)
+            if last:
+                tail_tanh(r - 1)
+            if live:
+                act(r, 2)
+                act(r, 3)
+            if r > 0 and not last:
+                tail_turn(r - 1)
+            if last:
+                ebank = gates.tile([P, CH], F32, name="ebank", tag="gate0")
+                for i in range(N_WARM_END):
+                    nc.tensor.matmul(out=ebank[:], lhsT=wz[:, 0:P], rhs=wz[:], start=True, stop=True)
+            for pc in plan.get(r, []):
+                prep_turn(pc)
+            if live and not last:
+                mm(r + 1, 2)
+                mm(r + 1, 3)
+            if r > 1:
+                tail_prod(r - 2)
+            if last:
+                tail_prod(r - 1)
+            for pc in plan.get(r - 1, []):
+                prep_copy(pc)
+            if not last:
+                do_rd(RD_POPS)
+            if live:
+                cell_c(r)
+            for pc in plan.get(r - 1, []):
+                prep_quant(pc)
+            if r < n - CAST_STOP:
+                do_cast(CAST_POPS, cq, "cast")
+
+        tail_turn(n - 1)
+        tail_tanh(n - 1)
+        do_rd(B * HID)
+        tail_prod(n - 1)
+        do_cast(len(sq), sq, "scast")
+        do_rd(B * HID)
+        do_cast(len(sq), sq, "scast")
+        do_cast(len(cq), cq, "cast")

@@ -23,16 +23,20 @@ NJ = 4
 CH = 512
 GATE_OF_POS = (0, 2, 1, 3)
 
-STEPS = [(0, 0), (1, 0), (0, 1), (1, 1), (0, 2), (1, 2), (0, 3), (0, 4), (1, 3), (0, 5), (0, 6), (1, 4), (0, 7), (1, 5), (1, 6), (1, 7)]
+STEPS = [(b, h, 0, 4) for b, h in ((0, 0), (1, 0), (0, 1), (1, 1), (0, 2), (1, 2), (0, 3), (0, 4), (1, 3), (0, 5), (0, 6), (1, 4), (0, 7), (1, 5), (1, 6), (1, 7))]
 BOUNDS = (0, 4, 7, 8)
-RD_BOUNDS = (0, 4, 6, 7, 8)
+RD_ROWS = (2, 2, 4)
 N_FINE = 3
 N_HEAD = 3
 PC_ON_SCALAR = (0, 1, 2, 3, 4, 5, 6)
-CAST_ON_SCALAR = ((0, 2, 0), (0, 2, 1), (0, 2, 2), (0, 3, 0), (0, 3, 1), (0, 3, 2), (1, 0, 1), (1, 1, 1), (1, 2, 1), (1, 3, 1))
+CAST_ON_SCALAR = ((0, 1, 0), (0, 1, 1), (0, 1, 2), (0, 2, 0), (0, 2, 1), (0, 2, 2), (0, 3, 0), (0, 3, 1), (0, 3, 2), (1, 0, 1), (1, 1, 1), (1, 2, 1), (1, 3, 1))
 RD_POPS = 1024
 CAST_POPS = 3
-CAST_STOP = 1
+ACC_FROM = 99
+FC_ON_GPSIMD = True
+IG_G_MIN = 1
+S_FILL = 3
+C_FIRST_FROM = 15
 N_WARM_END = 2
 LEAD = 4
 SMALL_DMA_AFTER = 2
@@ -140,10 +144,9 @@ def tile_rdecommunicationlstm_pa_kernel(tc, regime_vector, W_ih0, hh_gates, b_ih
             nc.vector.quantize_mx(out=codes[u][:, cols].bitcast(FP8X4), scales=scales[u][:, cols], in_=grouped[pc][:])
 
         nk = len(BOUNDS) - 1
-        nr = len(RD_BOUNDS) - 1
         big = [[keep.tile([P, NJ, P * (BOUNDS[k + 1] - BOUNDS[k])], F32, name="big%d_%d" % (b, k)) for k in range(nk)] for b in range(NB)]
         o8 = [[keep.tile([P, HID], FP8, name="o8_%d_%d" % (b, j)) for j in range(NJ)] for b in range(NB)]
-        stats = [keep.tile([P, nr, NJ], F32, name="stats%d" % b) for b in range(NB)]
+        stats = [keep.tile([P, nk, NJ], F32, name="stats%d" % b) for b in range(NB)]
         rscale = [keep.tile([P, NJ], F32, name="rscale%d" % b) for b in range(NB)]
         amax = [keep.tile([P, NJ], F32, name="amax%d" % b) for b in range(NB)]
         qscale = [keep.tile([P, NJ], F32, name="qscale%d" % b) for b in range(NB)]
@@ -153,40 +156,51 @@ def tile_rdecommunicationlstm_pa_kernel(tc, regime_vector, W_ih0, hh_gates, b_ih
         pg, av, cv, tv = {}, {}, {}, {}
 
         def mm(s, pos):
-            b, h = STEPS[s]
-            g = gates.tile([P, CH], F32, name="gate", tag="gate%d" % pos)
+            b, h, j0, nj = STEPS[s]
+            g = gates.tile([P, P * nj], F32, name="gate", tag="gate%d" % pos)
             cols = slice(P * pos, P * (pos + 1))
+            rows = slice(P * j0, P * (j0 + nj))
             nc.tensor.matmul_mx(out=g[:], lhsT=codes[("w", h)][:, cols].bitcast(FP8X4), lhsT_scale=scales[("w", h)][:, cols],
-                                rhs=codes[("x", b)][:].bitcast(FP8X4), rhs_scale=scales[("x", b)][:], start=True, stop=True)
+                                rhs=codes[("x", b)][:, rows].bitcast(FP8X4), rhs_scale=scales[("x", b)][:, rows], start=True, stop=True)
             pg[(s, pos)] = g
 
         def act(s, pos):
-            b, h = STEPS[s]
-            a = work.tile([P, CH], F32, name="act", tag="act%d" % pos)
+            b, h, j0, nj = STEPS[s]
+            a = work.tile([P, P * nj], F32, name="act", tag="act%d" % pos)
             col = GATE_OF_POS[pos] * NH + h
             nc.scalar.activation(out=a[:], in_=pg[(s, pos)][:], func=(ACT.Tanh if pos == 1 else ACT.Sigmoid), bias=bias[:, col : col + 1], scale=1.0)
             av[(s, pos)] = a
 
         def cell_ig(s):
-            ig = work.tile([P, CH], F32, name="ig", tag="ig")
-            nc.gpsimd.tensor_tensor(out=ig[:], in0=av[(s, 0)][:], in1=av[(s, 1)][:], op=ALU.mult)
+            ig = work.tile([P, P * STEPS[s][3]], F32, name="ig", tag="ig")
+            (nc.gpsimd if STEPS[s][3] >= IG_G_MIN else nc.vector).tensor_tensor(out=ig[:], in0=av[(s, 0)][:], in1=av[(s, 1)][:], op=ALU.mult)
             cv[(s, "ig")] = ig
 
         def cell_c(s):
-            b, h = STEPS[s]
-            c = work.tile([P, CH], F32, name="c", tag="c")
-            nc.vector.scalar_tensor_tensor(out=c[:], in0=av[(s, 2)][:], scalar=vcols[:, 96 + h : 97 + h], in1=cv[(s, "ig")][:], op0=ALU.mult, op1=ALU.add)
+            b, h, j0, nj = STEPS[s]
+            c = work.tile([P, P * nj], F32, name="c", tag="c")
+            if s < ACC_FROM:
+                nc.vector.scalar_tensor_tensor(out=c[:], in0=av[(s, 2)][:], scalar=vcols[:, 96 + h : 97 + h], in1=cv[(s, "ig")][:], op0=ALU.mult, op1=ALU.add)
+            elif FC_ON_GPSIMD:
+                nc.gpsimd.tensor_scalar(out=c[:], in0=av[(s, 2)][:], scalar1=vcols[:, 96 + h : 97 + h], scalar2=0.0, op0=ALU.mult, op1=ALU.add)
+            else:
+                nc.vector.tensor_scalar(out=c[:], in0=av[(s, 2)][:], scalar1=vcols[:, 96 + h : 97 + h], scalar2=None, op0=ALU.mult)
             cv[(s, "c")] = c
 
         def tail_turn(s):
             for key, src in (("cT", cv[(s, "c")]), ("oT", av[(s, 3)])):
-                bank = turn.tile([P, NJ, P], F32, name="tbank", tag="turn")
-                for j in range(NJ):
-                    nc.tensor.transpose(out=bank[:, j, :], in_=src[:, P * j : P * (j + 1)], identity=ident[:])
+                bank = turn.tile([P, STEPS[s][3], P], F32, name="tbank", tag="turn")
+                for j in range(STEPS[s][3]):
+                    cols = slice(P * j, P * (j + 1))
+                    if key == "cT" and s >= ACC_FROM:
+                        nc.tensor.matmul(out=bank[:, j, :], lhsT=cv[(s, "ig")][:, cols], rhs=ident[:], is_transpose=True, start=True, stop=False)
+                        nc.tensor.matmul(out=bank[:, j, :], lhsT=src[:, cols], rhs=ident[:], is_transpose=True, start=False, stop=True)
+                    else:
+                        nc.tensor.transpose(out=bank[:, j, :], in_=src[:, cols], identity=ident[:])
                 tv[(s, key)] = bank
 
         def tail_tanh(s):
-            th = work.tile([P, CH], F32, name="th", tag="th")
+            th = work.tile([P, P * STEPS[s][3]], F32, name="th", tag="th")
             nc.scalar.activation(out=th[:], in_=tv[(s, "cT")][:].rearrange("p j c -> p (j c)"), func=ACT.Tanh)
             tv[(s, "th")] = th
 
@@ -195,41 +209,35 @@ def tile_rdecommunicationlstm_pa_kernel(tc, regime_vector, W_ih0, hh_gates, b_ih
         cast_count = {}
 
         def tail_prod(s):
-            b, h = STEPS[s]
+            b, h, j0, nj = STEPS[s]
             k = max([i for i in range(nk) if BOUNDS[i] <= h])
             at = P * (h - BOUNDS[k])
-            nc.vector.tensor_tensor(out=big[b][k][:, :, at : at + P], in0=tv[(s, "oT")][:], in1=tv[(s, "th")][:].rearrange("p (j c) -> p j c", j=NJ), op=ALU.mult)
-            if h + 1 in RD_BOUNDS:
-                m = RD_BOUNDS.index(h + 1) - 1
-                if RD_BOUNDS[m] == BOUNDS[k] and h + 1 == BOUNDS[k + 1] and h + 1 - BOUNDS[k] == 1:
-                    rdq.append((b, NJ, m, k))
-                else:
-                    rdq.extend([(b, j, m, k) for j in range(NJ)])
+            nc.vector.tensor_tensor(out=big[b][k][:, j0 : j0 + nj, at : at + P], in0=tv[(s, "oT")][:], in1=tv[(s, "th")][:].rearrange("p (j c) -> p j c", j=nj), op=ALU.mult)
             if h + 1 in BOUNDS:
-                nc.sync.dma_start(out=o0v[b, :, :, P * BOUNDS[k] : P * BOUNDS[k + 1]], in_=big[b][k][:])
+                step = min(RD_ROWS[k], nj)
+                rdq.extend([(b, j, step, k, j0, nj) for j in range(j0, j0 + nj, step)])
+                nc.sync.dma_start(out=o0v[b, :, j0 : j0 + nj, P * BOUNDS[k] : P * BOUNDS[k + 1]], in_=big[b][k][:, j0 : j0 + nj, :])
 
         def do_rd(budget):
             spent = 0
             for i in range(len(rdq)):
                 if cur["rd"] >= len(rdq):
                     return
-                b, j, m, k = rdq[cur["rd"]]
-                lo, hi = P * (RD_BOUNDS[m] - BOUNDS[k]), P * (RD_BOUNDS[m + 1] - BOUNDS[k])
-                spent += (hi - lo) * (NJ if j == NJ else 1)
+                b, j, step, k, j0, nj = rdq[cur["rd"]]
+                spent += P * (BOUNDS[k + 1] - BOUNDS[k]) * step
                 if spent > budget:
                     return
                 cur["rd"] += 1
-                if j == NJ:
-                    nc.vector.tensor_reduce(out=stats[b][:, m, :], in_=big[b][k][:], axis=AX.X, op=ALU.max, apply_absolute_value=True)
-                else:
-                    nc.vector.tensor_reduce(out=stats[b][:, m, j : j + 1], in_=big[b][k][:, j, lo:hi], axis=AX.X, op=ALU.max, apply_absolute_value=True)
-                if m == nr - 2 and j >= NJ - 1:
-                    nc.vector.tensor_reduce(out=amax[b][:], in_=stats[b][:, 0 : nr - 1, :].rearrange("p m j -> p j m"), axis=AX.X, op=ALU.max)
-                    nc.vector.tensor_scalar(out=early[b][:], in0=amax[b][:], scalar1=1.0 / 448.0, scalar2=None, op0=ALU.mult)
-                if m == nr - 1 and j >= NJ - 1:
-                    nc.vector.scalar_tensor_tensor(out=qscale[b][:], in0=stats[b][:, nr - 1, :], scalar=1.0 / 448.0, in1=early[b][:], op0=ALU.mult, op1=ALU.max)
-                    nc.vector.reciprocal(out=rscale[b][:], in_=qscale[b][:])
-                    for jj in range(NJ):
+                js = slice(j, j + step)
+                jg = slice(j0, j0 + nj)
+                nc.vector.tensor_reduce(out=stats[b][:, k, js], in_=big[b][k][:, js, :], axis=AX.X, op=ALU.max, apply_absolute_value=True)
+                if k == nk - 2 and js.stop == jg.stop:
+                    nc.vector.tensor_reduce(out=amax[b][:, jg], in_=stats[b][:, 0 : nk - 1, jg].rearrange("p m j -> p j m"), axis=AX.X, op=ALU.max)
+                    nc.vector.tensor_scalar(out=early[b][:, jg], in0=amax[b][:, jg], scalar1=1.0 / 448.0, scalar2=None, op0=ALU.mult)
+                if k == nk - 1 and js.stop == jg.stop:
+                    nc.vector.scalar_tensor_tensor(out=qscale[b][:, jg], in0=stats[b][:, nk - 1, jg], scalar=1.0 / 448.0, in1=early[b][:, jg], op0=ALU.mult, op1=ALU.max)
+                    nc.vector.reciprocal(out=rscale[b][:, jg], in_=qscale[b][:, jg])
+                    for jj in range(j0, j0 + nj):
                         for kk in range(nk):
                             (sq if (b, jj, kk) in CAST_ON_SCALAR else cq).append((b, jj, kk))
 
@@ -272,57 +280,62 @@ def tile_rdecommunicationlstm_pa_kernel(tc, regime_vector, W_ih0, hh_gates, b_ih
             plan.setdefault(first_use[pc[0]] - LEAD + pc[1] // 2, []).append(pc)
         first_round = min([0] + [r for r in plan])
 
-        for r in range(first_round, n):
-            live = r >= 0
-            last = r == n - 1
+        e0 = min([s for s in range(n) if STEPS[s][3] < NJ] + [n])
+        th_mid, th_end = {}, {}
+        for s in range(n):
+            if s + 2 <= e0 and s + 2 < n:
+                th_mid.setdefault(s + 2, []).append(s)
+            else:
+                th_end.setdefault(min(s + 1, n - 1), []).append(s)
+        for r in range(first_round, n + 1):
+            live = 0 <= r < n
+            more = 0 <= r and r + 1 < n
             if live:
                 act(r, 0)
                 act(r, 1)
-            if live and not last:
+            if more:
                 mm(r + 1, 0)
                 mm(r + 1, 1)
             if live:
                 cell_ig(r)
-            if last:
-                tail_turn(r - 1)
-            if r > 1:
-                tail_tanh(r - 2)
-            if last:
-                tail_tanh(r - 1)
+            for s in th_mid.get(r, []):
+                tail_tanh(s)
             if live:
                 act(r, 2)
                 act(r, 3)
-            if r > 0 and not last:
+            if 0 <= r - 1 < e0 and r <= n - 1:
                 tail_turn(r - 1)
-            if last:
-                ebank = gates.tile([P, CH], F32, name="ebank", tag="gate0")
-                for i in range(N_WARM_END):
-                    nc.tensor.matmul(out=ebank[:], lhsT=wz[:, 0:P], rhs=wz[:], start=True, stop=True)
             for pc in plan.get(r, []):
                 prep_turn(pc)
-            if live and not last:
+            if more:
                 mm(r + 1, 2)
                 mm(r + 1, 3)
-            if r > 1:
-                tail_prod(r - 2)
-            if last:
-                tail_prod(r - 1)
+            for s in th_mid.get(r, []):
+                tail_prod(s)
+            for s in th_end.get(r - 1, []):
+                tail_prod(s)
+                if r == n:
+                    do_rd(B * HID)
             for pc in plan.get(r - 1, []):
                 prep_copy(pc)
-            if not last:
-                do_rd(RD_POPS)
-            if live:
+            if live and r >= C_FIRST_FROM:
+                cell_c(r)
+            do_rd(RD_POPS)
+            if live and r < C_FIRST_FROM:
                 cell_c(r)
             for pc in plan.get(r - 1, []):
                 prep_quant(pc)
-            if r < n - CAST_STOP:
-                do_cast(CAST_POPS, cq, "cast")
-
-        tail_turn(n - 1)
-        tail_tanh(n - 1)
-        do_rd(B * HID)
-        tail_prod(n - 1)
-        do_cast(len(sq), sq, "scast")
+            if live and (r >= e0 or r == n - 1):
+                if r == n - 1:
+                    ebank = gates.tile([P, CH], F32, name="ebank", tag="gate0")
+                    for i in range(N_WARM_END):
+                        nc.tensor.matmul(out=ebank[:], lhsT=wz[:, 0:P], rhs=wz[:], start=True, stop=True)
+                tail_turn(r)
+            for s in th_end.get(r, []):
+                if s == n - 1:
+                    do_cast(S_FILL, sq, "scast")
+                tail_tanh(s)
+            do_cast(CAST_POPS, cq, "cast")
         do_rd(B * HID)
         do_cast(len(sq), sq, "scast")
         do_cast(len(cq), cq, "cast")

@@ -275,9 +275,15 @@ def tile_rdecommunicationlstm_pa_kernel(tc, regime_vector, W_ih0, hh_gates, b_ih
                 mm(0, 2)
                 mm(0, 3)
 
+        late = pieces[n_head:]
+        turn_round = [0 for pc in late]
+        at = n
+        for i in reversed(range(len(late))):
+            at = min(first_use[late[i][0]] - LEAD + late[i][1] // 2, at - 1)
+            turn_round[i] = max(at, i - 2 if i < 2 else 0)
         plan = {}
-        for pc in pieces[n_head:]:
-            plan.setdefault(first_use[pc[0]] - LEAD + pc[1] // 2, []).append(pc)
+        for i in range(len(late)):
+            plan.setdefault(turn_round[i], []).append(late[i])
         first_round = min([0] + [r for r in plan])
 
         e0 = min([s for s in range(n) if STEPS[s][3] < NJ] + [n])
@@ -305,11 +311,13 @@ def tile_rdecommunicationlstm_pa_kernel(tc, regime_vector, W_ih0, hh_gates, b_ih
                 act(r, 3)
             if 0 <= r - 1 < e0 and r <= n - 1:
                 tail_turn(r - 1)
-            for pc in plan.get(r, []):
+            for pc in plan.get(r, [])[:1]:
                 prep_turn(pc)
             if more:
                 mm(r + 1, 2)
                 mm(r + 1, 3)
+            for pc in plan.get(r, [])[1:]:
+                prep_turn(pc)
             for s in th_mid.get(r, []):
                 tail_prod(s)
             for s in th_end.get(r - 1, []):

@@ -55,7 +55,7 @@ def tile_rdecommunicationlstm_pa_kernel(tc, regime_vector, W_ih0, hh_gates, b_ih
         work = ctx.enter_context(tc.tile_pool(name="work", bufs=3))
         gates = ctx.enter_context(tc.psum_pool(name="gates", bufs=1))
         turn = ctx.enter_context(tc.psum_pool(name="turn", bufs=4))
-        ctx.enter_context(tc.manual_schedule())
+        ctx.enter_context(tc.manual_schedule(engines={mybir.EngineType.PE, mybir.EngineType.SP}))
 
         units, first_use = [], {}
         for s in range(n):

@@ -23,7 +23,7 @@ NJ = 4
 CH = 512
 GATE_OF_POS = (0, 2, 1, 3)
 
-STEPS = [(b, h, 0, 4) for b, h in ((0, 0), (1, 0), (0, 1), (1, 1), (0, 2), (1, 2), (0, 3), (0, 4), (1, 3), (0, 5), (0, 6), (1, 4), (0, 7), (1, 5), (1, 6), (1, 7))]
+STEPS = [(b, h, 0, 4) for b, h in ((0, 0), (1, 0), (0, 1), (1, 1), (0, 2), (1, 2), (0, 3), (0, 4), (1, 3), (0, 5), (0, 6), (1, 4), (0, 7), (1, 5), (1, 6))] + [(1, 7, 0, 2), (1, 7, 2, 1), (1, 7, 3, 1)]
 BOUNDS = (0, 4, 7, 8)
 RD_ROWS = (2, 2, 4)
 N_FINE = 3
@@ -35,7 +35,7 @@ CAST_POPS = 3
 ACC_FROM = 99
 FC_ON_GPSIMD = True
 IG_G_MIN = 1
-S_FILL = 3
+S_FILL = 1
 C_FIRST_FROM = 15
 N_WARM_END = 2
 LEAD = 4

from contextlib import ExitStack

import concourse.mybir as mybir
from concourse.masks import make_identity

F32 = mybir.dt.float32
BF16 = mybir.dt.bfloat16
U32 = mybir.dt.uint32
U8 = mybir.dt.uint8
FP8 = mybir.dt.float8_e4m3fn
FP8X4 = mybir.dt.float8_e4m3fn_x4
ACT = mybir.ActivationFunctionType
ALU = mybir.AluOpType
AX = mybir.AxisListType

B, IN, HID = 1024, 512, 1024
FLOPS = 2 * B * 4 * HID * IN

P = 128
NB = 2
NH = 8
NJ = 4
CH = 512
GATE_OF_POS = (0, 2, 1, 3)

STEPS = [(b, h, 0, 4) for b, h in ((0, 0), (1, 0), (0, 1), (1, 1), (0, 2), (1, 2), (0, 3), (0, 4), (1, 3), (0, 5), (0, 6), (1, 4), (0, 7), (1, 5), (1, 6))] + [(1, 7, 0, 2), (1, 7, 2, 1), (1, 7, 3, 1)]
BOUNDS = (0, 4, 7, 8)
RD_ROWS = (2, 2, 4)
N_FINE = 3
N_HEAD = 3
PC_ON_SCALAR = (0, 1, 2, 3, 4, 5, 6)
CAST_ON_SCALAR = ((0, 1, 0), (0, 1, 1), (0, 1, 2), (0, 2, 0), (0, 2, 1), (0, 2, 2), (0, 3, 0), (0, 3, 1), (0, 3, 2), (1, 0, 1), (1, 1, 1), (1, 2, 1), (1, 3, 1))
RD_POPS = 1024
CAST_POPS = 3
ACC_FROM = 99
FC_ON_GPSIMD = True
IG_G_MIN = 1
S_FILL = 1
C_FIRST_FROM = 15
N_WARM_END = 2
LEAD = 4
SMALL_DMA_AFTER = 2
SMALL_AFTER = 4
WARM_UNTIL = 6
N_WARM = 6
WARM_EVERY = 2


def tile_rdecommunicationlstm_pa_kernel(tc, regime_vector, W_ih0, hh_gates, b_ih0, b_hh0, c_init, out_0, out_1):
    nc = tc.nc
    n = len(STEPS)
    with ExitStack() as ctx:
        const = ctx.enter_context(tc.tile_pool(name="const", bufs=1))
        keep = ctx.enter_context(tc.tile_pool(name="keep", bufs=1))
        work = ctx.enter_context(tc.tile_pool(name="work", bufs=3))
        gates = ctx.enter_context(tc.psum_pool(name="gates", bufs=1))
        turn = ctx.enter_context(tc.psum_pool(name="turn", bufs=4))
        ctx.enter_context(tc.manual_schedule(engines={mybir.EngineType.PE, mybir.EngineType.SP}))

        units, first_use = [], {}
        for s in range(n):
            for u in (("x", STEPS[s][0]), ("w", STEPS[s][1])):
                if u not in units:
                    units.append(u)
                    first_use[u] = s
        pieces = []
        for i in range(len(units)):
            nt = 1 if i < N_FINE else 2
            pieces.extend([(units[i], t0, nt) for t0 in range(0, 4, nt)])
        n_head = 4 * N_FINE + 2 * (N_HEAD - N_FINE)

        xv = regime_vector.rearrange("(b f t p) k -> b f p t k", b=NB, f=2, t=2, p=P)
        wv = W_ih0.rearrange("(t f h p) k -> h f p t k", t=2, f=2, h=NH, p=P)
        vrows = const.tile([P, P], BF16, name="vrows")
        nc.vector.memset(vrows[96:128, :], 0.0)
        raw = {}
        for pc in pieces:
            if pieces.index(pc) == SMALL_DMA_AFTER:
                nc.sync.dma_start(out=vrows[0:32, :], in_=hh_gates.rearrange("(c p) -> c p", p=P))
                nc.sync.dma_start(out=vrows[32:64, :], in_=b_ih0.rearrange("(c p) -> c p", p=P))
                nc.sync.dma_start(out=vrows[64:96, :], in_=b_hh0.rearrange("(c p) -> c p", p=P))
                nc.sync.dma_start(out=vrows[96:104, :], in_=c_init.rearrange("(c p) -> c p", p=P))
            u, t0, nt = pc
            r = keep.tile([P, nt, IN], BF16, name="raw_%s%d_%d" % (u[0], u[1], t0))
            view = xv if u[0] == "x" else wv
            nc.sync.dma_start(out=r[:], in_=view[u[1], t0 // 2, :, t0 % 2 : t0 % 2 + nt, :])
            raw[pc] = r

        wz = const.tile([P, CH], BF16, name="wz")
        nc.vector.memset(wz[:], 0.0)
        wbank = gates.tile([P, CH], F32, name="wbank", tag="gate3")

        def warm_pass():
            nc.tensor.matmul(out=wbank[:], lhsT=wz[:, 0:P], rhs=wz[:], start=True, stop=True)

        for i in range(N_WARM):
            warm_pass()
        zero = const.tile([P, 1], F32, name="zero")
        nc.vector.memset(zero[:], 0.0)
        warm = const.tile([P, 1], F32, name="warm")
        nc.scalar.activation(out=warm[:], in_=zero[:], func=ACT.Sigmoid)
        ident = const.tile([P, P], F32, name="ident")
        make_identity(nc, ident[:])
        ident_bf = const.tile([P, P], BF16, name="ident_bf")
        make_identity(nc, ident_bf[:])
        vcols = const.tile([P, P], F32, name="vcols")
        bsum = const.tile([P, 32], F32, name="bsum")
        bias = const.tile([P, 32], F32, name="bias")

        def small_vectors():
            bank = turn.tile([P, P], BF16, name="vbank", tag="turn")
            nc.tensor.transpose(out=bank[:], in_=vrows[:], identity=ident_bf[:])
            nc.vector.tensor_copy(out=vcols[:], in_=bank[:])
            nc.vector.tensor_tensor(out=bsum[:], in0=vcols[:, 32:64], in1=vcols[:, 64:96], op=ALU.add)
            nc.vector.tensor_tensor(out=bias[:], in0=bsum[:], in1=vcols[:, 0:32], op=ALU.add)

        grouped, codes, scales, banks = {}, {}, {}, {}
        for u in units:
            codes[u] = keep.tile([P, CH], U32, name="codes_%s%d" % u, align_bytes=64)
            scales[u] = keep.tile([P, CH], U8, name="scales_%s%d" % u, align_bytes=64)

        def prep_turn(pc):
            nt = pc[2]
            bank = turn.tile([P, 2, nt, P], F32, name="pbank", tag="turn")
            words = raw[pc][:].rearrange("p t k -> p (t k)").bitcast(F32)
            for t in range(nt):
                for w in range(2):
                    nc.tensor.transpose(out=bank[:, w, t, :], in_=words[:, 256 * t + w : 256 * (t + 1) : 2], identity=ident[:])
            banks[pc] = bank

        def prep_copy(pc):
            g = work.tile([P, pc[2] * CH], BF16, name="grouped", tag="grouped", bufs=4, align_bytes=64)
            dst = g[:].bitcast(F32).rearrange("p (n w) -> p n w", w=2)
            src = banks[pc][:].rearrange("p w t r -> p (t r) w")
            if pieces.index(pc) in PC_ON_SCALAR:
                nc.scalar.copy(out=dst, in_=src)
            else:
                nc.vector.tensor_copy(out=dst, in_=src)
            grouped[pc] = g

        def prep_quant(pc):
            u, t0, nt = pc
            cols = slice(P * t0, P * (t0 + nt))
            nc.vector.quantize_mx(out=codes[u][:, cols].bitcast(FP8X4), scales=scales[u][:, cols], in_=grouped[pc][:])

        nk = len(BOUNDS) - 1
        big = [[keep.tile([P, NJ, P * (BOUNDS[k + 1] - BOUNDS[k])], F32, name="big%d_%d" % (b, k)) for k in range(nk)] for b in range(NB)]
        o8 = [[keep.tile([P, HID], FP8, name="o8_%d_%d" % (b, j)) for j in range(NJ)] for b in range(NB)]
        stats = [keep.tile([P, nk, NJ], F32, name="stats%d" % b) for b in range(NB)]
        rscale = [keep.tile([P, NJ], F32, name="rscale%d" % b) for b in range(NB)]
        amax = [keep.tile([P, NJ], F32, name="amax%d" % b) for b in range(NB)]
        qscale = [keep.tile([P, NJ], F32, name="qscale%d" % b) for b in range(NB)]
        early = [keep.tile([P, NJ], F32, name="early%d" % b) for b in range(NB)]
        o0v = out_0.rearrange("(b j p) c -> b p j c", b=NB, j=NJ, p=P)
        o1v = out_1.rearrange("(b j p) c -> b j p c", b=NB, j=NJ, p=P)
        pg, av, cv, tv = {}, {}, {}, {}

        def mm(s, pos):
            b, h, j0, nj = STEPS[s]
            g = gates.tile([P, P * nj], F32, name="gate", tag="gate%d" % pos)
            cols = slice(P * pos, P * (pos + 1))
            rows = slice(P * j0, P * (j0 + nj))
            nc.tensor.matmul_mx(out=g[:], lhsT=codes[("w", h)][:, cols].bitcast(FP8X4), lhsT_scale=scales[("w", h)][:, cols],
                                rhs=codes[("x", b)][:, rows].bitcast(FP8X4), rhs_scale=scales[("x", b)][:, rows], start=True, stop=True)
            pg[(s, pos)] = g

        def act(s, pos):
            b, h, j0, nj = STEPS[s]
            a = work.tile([P, P * nj], F32, name="act", tag="act%d" % pos)
            col = GATE_OF_POS[pos] * NH + h
            nc.scalar.activation(out=a[:], in_=pg[(s, pos)][:], func=(ACT.Tanh if pos == 1 else ACT.Sigmoid), bias=bias[:, col : col + 1], scale=1.0)
            av[(s, pos)] = a

        def cell_ig(s):
            ig = work.tile([P, P * STEPS[s][3]], F32, name="ig", tag="ig")
            (nc.gpsimd if STEPS[s][3] >= IG_G_MIN else nc.vector).tensor_tensor(out=ig[:], in0=av[(s, 0)][:], in1=av[(s, 1)][:], op=ALU.mult)
            cv[(s, "ig")] = ig

        def cell_c(s):
            b, h, j0, nj = STEPS[s]
            c = work.tile([P, P * nj], F32, name="c", tag="c")
            if s < ACC_FROM:
                nc.vector.scalar_tensor_tensor(out=c[:], in0=av[(s, 2)][:], scalar=vcols[:, 96 + h : 97 + h], in1=cv[(s, "ig")][:], op0=ALU.mult, op1=ALU.add)
            elif FC_ON_GPSIMD:
                nc.gpsimd.tensor_scalar(out=c[:], in0=av[(s, 2)][:], scalar1=vcols[:, 96 + h : 97 + h], scalar2=0.0, op0=ALU.mult, op1=ALU.add)
            else:
                nc.vector.tensor_scalar(out=c[:], in0=av[(s, 2)][:], scalar1=vcols[:, 96 + h : 97 + h], scalar2=None, op0=ALU.mult)
            cv[(s, "c")] = c

        def tail_turn(s):
            for key, src in (("cT", cv[(s, "c")]), ("oT", av[(s, 3)])):
                bank = turn.tile([P, STEPS[s][3], P], F32, name="tbank", tag="turn")
                for j in range(STEPS[s][3]):
                    cols = slice(P * j, P * (j + 1))
                    if key == "cT" and s >= ACC_FROM:
                        nc.tensor.matmul(out=bank[:, j, :], lhsT=cv[(s, "ig")][:, cols], rhs=ident[:], is_transpose=True, start=True, stop=False)
                        nc.tensor.matmul(out=bank[:, j, :], lhsT=src[:, cols], rhs=ident[:], is_transpose=True, start=False, stop=True)
                    else:
                        nc.tensor.transpose(out=bank[:, j, :], in_=src[:, cols], identity=ident[:])
                tv[(s, key)] = bank

        def tail_tanh(s):
            th = work.tile([P, P * STEPS[s][3]], F32, name="th", tag="th")
            nc.scalar.activation(out=th[:], in_=tv[(s, "cT")][:].rearrange("p j c -> p (j c)"), func=ACT.Tanh)
            tv[(s, "th")] = th

        rdq, cq, sq = [], [], []
        cur = {"rd": 0, "cast": 0, "scast": 0}
        cast_count = {}

        def tail_prod(s):
            b, h, j0, nj = STEPS[s]
            k = max([i for i in range(nk) if BOUNDS[i] <= h])
            at = P * (h - BOUNDS[k])
            nc.vector.tensor_tensor(out=big[b][k][:, j0 : j0 + nj, at : at + P], in0=tv[(s, "oT")][:], in1=tv[(s, "th")][:].rearrange("p (j c) -> p j c", j=nj), op=ALU.mult)
            if h + 1 in BOUNDS:
                step = min(RD_ROWS[k], nj)
                rdq.extend([(b, j, step, k, j0, nj) for j in range(j0, j0 + nj, step)])
                nc.sync.dma_start(out=o0v[b, :, j0 : j0 + nj, P * BOUNDS[k] : P * BOUNDS[k + 1]], in_=big[b][k][:, j0 : j0 + nj, :])

        def do_rd(budget):
            spent = 0
            for i in range(len(rdq)):
                if cur["rd"] >= len(rdq):
                    return
                b, j, step, k, j0, nj = rdq[cur["rd"]]
                spent += P * (BOUNDS[k + 1] - BOUNDS[k]) * step
                if spent > budget:
                    return
                cur["rd"] += 1
                js = slice(j, j + step)
                jg = slice(j0, j0 + nj)
                nc.vector.tensor_reduce(out=stats[b][:, k, js], in_=big[b][k][:, js, :], axis=AX.X, op=ALU.max, apply_absolute_value=True)
                if k == nk - 2 and js.stop == jg.stop:
                    nc.vector.tensor_reduce(out=amax[b][:, jg], in_=stats[b][:, 0 : nk - 1, jg].rearrange("p m j -> p j m"), axis=AX.X, op=ALU.max)
                    nc.vector.tensor_scalar(out=early[b][:, jg], in0=amax[b][:, jg], scalar1=1.0 / 448.0, scalar2=None, op0=ALU.mult)
                if k == nk - 1 and js.stop == jg.stop:
                    nc.vector.scalar_tensor_tensor(out=qscale[b][:, jg], in0=stats[b][:, nk - 1, jg], scalar=1.0 / 448.0, in1=early[b][:, jg], op0=ALU.mult, op1=ALU.max)
                    nc.vector.reciprocal(out=rscale[b][:, jg], in_=qscale[b][:, jg])
                    for jj in range(j0, j0 + nj):
                        for kk in range(nk):
                            (sq if (b, jj, kk) in CAST_ON_SCALAR else cq).append((b, jj, kk))

        def do_cast(count, queue, key):
            for i in range(count):
                if cur[key] >= len(queue):
                    return
                b, j, k = queue[cur[key]]
                cur[key] += 1
                dst = o8[b][j][:, P * BOUNDS[k] : P * BOUNDS[k + 1]]
                if key == "scast":
                    nc.scalar.activation(out=dst, in_=big[b][k][:, j, :], func=ACT.Identity, scale=rscale[b][:, j : j + 1], bias=zero[:, 0:1], saturate=False)
                else:
                    nc.vector.tensor_scalar(out=dst, in0=big[b][k][:, j, :], scalar1=rscale[b][:, j : j + 1], scalar2=None, op0=ALU.mult, saturate=False)
                cast_count[(b, j)] = cast_count.get((b, j), 0) + 1
                if cast_count[(b, j)] == nk:
                    nc.sync.dma_start(out=o1v[b, j, :, :], in_=o8[b][j][:].bitcast(U8))

        head = pieces[:n_head]
        for i in range(n_head + 2):
            if i < n_head:
                prep_turn(head[i])
                if i < WARM_UNTIL and i % WARM_EVERY == WARM_EVERY - 1:
                    warm_pass()
            if 1 <= i <= n_head:
                prep_copy(head[i - 1])
            if i >= 2:
                prep_quant(head[i - 2])
            if i == SMALL_AFTER:
                small_vectors()
            if i == 7:
                mm(0, 0)
                mm(0, 1)
            if i == 11:
                mm(0, 2)
                mm(0, 3)

        late = pieces[n_head:]
        turn_round = [0 for pc in late]
        at = n
        for i in reversed(range(len(late))):
            at = min(first_use[late[i][0]] - LEAD + late[i][1] // 2, at - 1)
            turn_round[i] = max(at, i - 2 if i < 2 else 0)
        plan = {}
        for i in range(len(late)):
            plan.setdefault(turn_round[i], []).append(late[i])
        first_round = min([0] + [r for r in plan])

        e0 = min([s for s in range(n) if STEPS[s][3] < NJ] + [n])
        th_mid, th_end = {}, {}
        for s in range(n):
            if s + 2 <= e0 and s + 2 < n:
                th_mid.setdefault(s + 2, []).append(s)
            else:
                th_end.setdefault(min(s + 1, n - 1), []).append(s)
        for r in range(first_round, n + 1):
            live = 0 <= r < n
            more = 0 <= r and r + 1 < n
            if live:
                act(r, 0)
                act(r, 1)
            if more:
                mm(r + 1, 0)
                mm(r + 1, 1)
            if live:
                cell_ig(r)
            for s in th_mid.get(r, []):
                tail_tanh(s)
            if live:
                act(r, 2)
                act(r, 3)
            if 0 <= r - 1 < e0 and r <= n - 1:
                tail_turn(r - 1)
            for pc in plan.get(r, [])[:1]:
                prep_turn(pc)
            if more:
                mm(r + 1, 2)
                mm(r + 1, 3)
            for pc in plan.get(r, [])[1:]:
                prep_turn(pc)
            for s in th_mid.get(r, []):
                tail_prod(s)
            for s in th_end.get(r - 1, []):
                tail_prod(s)
                if r == n:
                    do_rd(B * HID)
            for pc in plan.get(r - 1, []):
                prep_copy(pc)
            if live and r >= C_FIRST_FROM:
                cell_c(r)
            do_rd(RD_POPS)
            if live and r < C_FIRST_FROM:
                cell_c(r)
            for pc in plan.get(r - 1, []):
                prep_quant(pc)
            if live and (r >= e0 or r == n - 1):
                if r == n - 1:
                    ebank = gates.tile([P, CH], F32, name="ebank", tag="gate0")
                    for i in range(N_WARM_END):
                        nc.tensor.matmul(out=ebank[:], lhsT=wz[:, 0:P], rhs=wz[:], start=True, stop=True)
                tail_turn(r)
            for s in th_end.get(r, []):
                if s == n - 1:
                    do_cast(S_FILL, sq, "scast")
                tail_tanh(s)
            do_cast(CAST_POPS, cq, "cast")
        do_rd(B * HID)
        do_cast(len(sq), sq, "scast")
        do_cast(len(cq), cq, "cast")
